import numpy as np
import ml_dtypes

BF16 = ml_dtypes.bfloat16


def bf(x):
    return np.asarray(x, np.float32).astype(BF16)


def f32(x):
    return np.asarray(x, np.float32)


def f64(x):
    return np.asarray(x).astype(np.float64)


def striped(idx):
    return np.tile(idx.reshape(-1, 16).T, (8, 1))


C, S, N, A, R, T, Q = 256, 256, 256, 8, 32, 512, 16


def setup_inputs():
    bins = np.random.permutation(np.arange(Q) % A)
    tok = np.repeat(bins, T // Q)
    mask = np.repeat(np.arange(A), R)[:, None] == tok[None, :]
    s = 0.5 + np.random.uniform(size=A)
    scale = np.tile(np.repeat(s, R)[None, :], (C, 1))
    return {"x": bf(np.random.standard_normal((C, T))), "a_w": bf(np.random.standard_normal((C, N)) / np.sqrt(C)), "b_pool": f32(np.random.standard_normal((C, S)) / np.sqrt(R)), "scale": f32(scale), "mask": f32(mask), "offs": striped(np.random.permutation(S)[:N])}


def reference(x, a_w, b_pool, scale, mask, offs):
    idx = offs[:16].T.reshape(-1)
    bw = f64(b_pool)[:, idx] * f64(scale)
    dm = (f64(a_w).T @ f64(x)) * f64(mask)
    return bw @ dm

@@ -1,0 +1,85 @@
+import concourse.mybir as mybir
+from concourse.masks import make_identity
+
+P = 128
+C = 256
+S = 256
+N = 256
+T = 512
+BLOCKS = 2
+
+FLOPS = 2 * C * N * T + 2 * N * C * T
+
+BF16, F32, U16 = mybir.dt.bfloat16, mybir.dt.float32, mybir.dt.uint16
+MULT = mybir.AluOpType.mult
+
+
+def tile_qkvparallellinearwithlora_kernel(tc, x, a_w, b_pool, scale, mask, offs, out):
+    nc = tc.nc
+    with (
+        tc.tile_pool(name="held", bufs=1) as held,
+        tc.psum_pool(name="psum", bufs=1) as psum,
+    ):
+        offsets = held.tile([P, N // 16], U16, name="offsets")
+        nc.sync.dma_start(offsets[:], offs)
+
+        queues = [nc.sync, nc.scalar]
+        pool_t, scale_t, a_t, x_t, mask_t = [], [], [], [], []
+        for tiles, source, width, dtype, label in (
+            (pool_t, b_pool, S, F32, "pool"),
+            (scale_t, scale, N, F32, "scale"),
+            (a_t, a_w, N, BF16, "a"),
+            (x_t, x, T, BF16, "x"),
+            (mask_t, mask, T, F32, "mask"),
+        ):
+            for b in range(BLOCKS):
+                block = held.tile([P, width], dtype, name=f"{label}{b}")
+                queues[b].dma_start(block[:], source[b * P : (b + 1) * P, :])
+                tiles.append(block)
+
+        identity = held.tile([P, P], F32, name="identity")
+        make_identity(nc, identity[:])
+
+        bwT = []
+        for cb in range(BLOCKS):
+            bw = held.tile([P, N], F32, name=f"bw{cb}")
+            nc.vector.tensor_tensor(bw[:], pool_t[cb][:].indirect(offsets[:]), scale_t[cb][:], MULT)
+            flipped = psum.tile([P, N], F32, name=f"flipped{cb}")
+            for jb in range(BLOCKS):
+                cols = slice(jb * P, (jb + 1) * P)
+                nc.tensor.transpose(flipped[:, cols], bw[:, cols], identity[:])
+            rounded = held.tile([P, N], BF16, name=f"bwT{cb}")
+            nc.scalar.copy(rounded[:], flipped[:])
+            bwT.append(rounded)
+
+        dm = []
+        for jb in range(BLOCKS):
+            shrunk = psum.tile([P, T], F32, name=f"shrunk{jb}")
+            for kb in range(BLOCKS):
+                nc.tensor.matmul(
+                    shrunk[:],
+                    a_t[kb][:, jb * P : (jb + 1) * P],
+                    x_t[kb][:],
+                    start=(kb == 0),
+                    stop=(kb == BLOCKS - 1),
+                )
+            kept = held.tile([P, T], BF16, name=f"dm{jb}")
+            nc.vector.tensor_tensor(kept[:], shrunk[:], mask_t[jb][:], MULT)
+            dm.append(kept)
+
+        for cb in range(BLOCKS):
+            expanded = psum.tile([P, T], F32, name=f"expanded{cb}")
+            for jb in range(BLOCKS):
+                nc.tensor.matmul(
+                    expanded[:],
+                    bwT[cb][:, jb * P : (jb + 1) * P],
+                    dm[jb][:],
+                    start=(jb == 0),
+                    stop=(jb == BLOCKS - 1),
+                )
+            result = held.tile([P, T], F32, name=f"result{cb}")
+            if cb == 0:
+                nc.vector.tensor_copy(result[:], expanded[:])
+            else:
+                nc.scalar.copy(result[:], expanded[:])
+            queues[cb].dma_start(out[cb * P : (cb + 1) * P, :], result[:])

@@ -8,6 +8,8 @@ N = 256
 T = 512
 BLOCKS = 2
 
+WARM_UP_MATMULS = 6
+
 FLOPS = 2 * C * N * T + 2 * N * C * T
 
 BF16, F32, U16 = mybir.dt.bfloat16, mybir.dt.float32, mybir.dt.uint16
@@ -39,6 +41,12 @@ def tile_qkvparallellinearwithlora_kernel(tc, x, a_w, b_pool, scale, mask, offs,
 
         identity = held.tile([P, P], F32, name="identity")
         make_identity(nc, identity[:])
+
+        zeros = held.tile([P, T], BF16, name="zeros")
+        nc.vector.memset(zeros[:], 0.0)
+        idle_product = psum.tile([P, T], F32, name="idle_product")
+        for i in range(WARM_UP_MATMULS):
+            nc.tensor.matmul(idle_product[:], zeros[:, :P], zeros[:], start=True, stop=True)
 
         bwT = []
         for cb in range(BLOCKS):

@@ -7,13 +7,18 @@ S = 256
 N = 256
 T = 512
 BLOCKS = 2
-
-WARM_UP_MATMULS = 6
+WARM_UP_MATMULS = 4
+CHUNKS = 2
+TQ = T // CHUNKS
 
 FLOPS = 2 * C * N * T + 2 * N * C * T
 
 BF16, F32, U16 = mybir.dt.bfloat16, mybir.dt.float32, mybir.dt.uint16
 MULT = mybir.AluOpType.mult
+
+
+def blocked(rows):
+    return rows.rearrange("(b p) w -> p b w", p=P)
 
 
 def tile_qkvparallellinearwithlora_kernel(tc, x, a_w, b_pool, scale, mask, offs, out):
@@ -23,21 +28,21 @@ def tile_qkvparallellinearwithlora_kernel(tc, x, a_w, b_pool, scale, mask, offs,
         tc.psum_pool(name="psum", bufs=1) as psum,
     ):
         offsets = held.tile([P, N // 16], U16, name="offsets")
-        nc.sync.dma_start(offsets[:], offs)
+        pool_t = [held.tile([P, S], F32, name=f"pool{cb}") for cb in range(BLOCKS)]
+        scale_t = [held.tile([P, N], F32, name=f"scale{cb}") for cb in range(BLOCKS)]
+        a_t = held.tile([P, BLOCKS, N], BF16, name="a_t")
+        x_t = held.tile([P, BLOCKS, T], BF16, name="x_t")
+        mask_t = [held.tile([P, BLOCKS, TQ], F32, name=f"mask{q}") for q in range(CHUNKS)]
 
-        queues = [nc.sync, nc.scalar]
-        pool_t, scale_t, a_t, x_t, mask_t = [], [], [], [], []
-        for tiles, source, width, dtype, label in (
-            (pool_t, b_pool, S, F32, "pool"),
-            (scale_t, scale, N, F32, "scale"),
-            (a_t, a_w, N, BF16, "a"),
-            (x_t, x, T, BF16, "x"),
-            (mask_t, mask, T, F32, "mask"),
-        ):
-            for b in range(BLOCKS):
-                block = held.tile([P, width], dtype, name=f"{label}{b}")
-                queues[b].dma_start(block[:], source[b * P : (b + 1) * P, :])
-                tiles.append(block)
+        nc.sync.dma_start(offsets[:], offs)
+        nc.sync.dma_start(pool_t[0][:], b_pool[0:P, :])
+        nc.scalar.dma_start(scale_t[0][:], scale[0:P, :])
+        nc.sync.dma_start(a_t[:], blocked(a_w))
+        nc.scalar.dma_start(x_t[:], blocked(x))
+        nc.sync.dma_start(pool_t[1][:], b_pool[P : 2 * P, :])
+        nc.scalar.dma_start(scale_t[1][:], scale[P : 2 * P, :])
+        nc.sync.dma_start(mask_t[0][:], blocked(mask)[:, :, 0:TQ])
+        nc.scalar.dma_start(mask_t[1][:], blocked(mask)[:, :, TQ:T])
 
         identity = held.tile([P, P], F32, name="identity")
         make_identity(nc, identity[:])
@@ -48,46 +53,55 @@ def tile_qkvparallellinearwithlora_kernel(tc, x, a_w, b_pool, scale, mask, offs,
         for i in range(WARM_UP_MATMULS):
             nc.tensor.matmul(idle_product[:], zeros[:, :P], zeros[:], start=True, stop=True)
 
-        bwT = []
-        for cb in range(BLOCKS):
-            bw = held.tile([P, N], F32, name=f"bw{cb}")
-            nc.vector.tensor_tensor(bw[:], pool_t[cb][:].indirect(offsets[:]), scale_t[cb][:], MULT)
-            flipped = psum.tile([P, N], F32, name=f"flipped{cb}")
+        flipped = psum.tile([P, BLOCKS, BLOCKS, P], F32, name="flipped")
+        bwT = held.tile([P, BLOCKS, BLOCKS, P], BF16, name="bwT")
+
+        def look_up(cb):
+            bw = held.tile([P, BLOCKS, P], F32, name=f"bw{cb}")
+            nc.vector.tensor_tensor(
+                bw[:].rearrange("p b j -> p (b j)"), pool_t[cb][:].indirect(offsets[:]), scale_t[cb][:], MULT
+            )
             for jb in range(BLOCKS):
-                cols = slice(jb * P, (jb + 1) * P)
-                nc.tensor.transpose(flipped[:, cols], bw[:, cols], identity[:])
-            rounded = held.tile([P, N], BF16, name=f"bwT{cb}")
-            nc.scalar.copy(rounded[:], flipped[:])
-            bwT.append(rounded)
+                nc.tensor.transpose(flipped[:, cb, jb, :], bw[:, jb, :], identity[:])
+            nc.scalar.copy(bwT[:, cb], flipped[:, cb])
+
+        def shrink(q):
+            shrunk = psum.tile([P, BLOCKS, TQ], F32, name=f"shrunk{q}")
+            for jb in range(BLOCKS):
+                for kb in range(BLOCKS):
+                    nc.tensor.matmul(
+                        shrunk[:, jb, :],
+                        a_t[:, kb, jb * P : (jb + 1) * P],
+                        x_t[:, kb, q * TQ : (q + 1) * TQ],
+                        start=(kb == 0),
+                        stop=(kb == BLOCKS - 1),
+                    )
+            return shrunk
+
+        look_up(0)
+        shrunk = [shrink(q) for q in range(CHUNKS)]
+        look_up(1)
 
         dm = []
-        for jb in range(BLOCKS):
-            shrunk = psum.tile([P, T], F32, name=f"shrunk{jb}")
-            for kb in range(BLOCKS):
-                nc.tensor.matmul(
-                    shrunk[:],
-                    a_t[kb][:, jb * P : (jb + 1) * P],
-                    x_t[kb][:],
-                    start=(kb == 0),
-                    stop=(kb == BLOCKS - 1),
-                )
-            kept = held.tile([P, T], BF16, name=f"dm{jb}")
-            nc.vector.tensor_tensor(kept[:], shrunk[:], mask_t[jb][:], MULT)
+        for q in range(CHUNKS):
+            kept = held.tile([P, BLOCKS, TQ], BF16, name=f"dm{q}")
+            nc.vector.tensor_tensor(kept[:], shrunk[q][:], mask_t[q][:], MULT)
             dm.append(kept)
 
-        for cb in range(BLOCKS):
-            expanded = psum.tile([P, T], F32, name=f"expanded{cb}")
-            for jb in range(BLOCKS):
-                nc.tensor.matmul(
-                    expanded[:],
-                    bwT[cb][:, jb * P : (jb + 1) * P],
-                    dm[jb][:],
-                    start=(jb == 0),
-                    stop=(jb == BLOCKS - 1),
-                )
-            result = held.tile([P, T], F32, name=f"result{cb}")
-            if cb == 0:
-                nc.vector.tensor_copy(result[:], expanded[:])
-            else:
-                nc.scalar.copy(result[:], expanded[:])
-            queues[cb].dma_start(out[cb * P : (cb + 1) * P, :], result[:])
+        for q in range(CHUNKS):
+            for cb in range(BLOCKS):
+                expanded = psum.tile([P, TQ], F32, name=f"expanded{q}{cb}")
+                for jb in range(BLOCKS):
+                    nc.tensor.matmul(
+                        expanded[:],
+                        bwT[:, cb, jb, :],
+                        dm[q][:, jb, :],
+                        start=(jb == 0),
+                        stop=(jb == BLOCKS - 1),
+                    )
+                result = held.tile([P, TQ], F32, name=f"result{q}{cb}")
+                if cb == 0:
+                    nc.vector.tensor_copy(result[:], expanded[:])
+                else:
+                    nc.scalar.copy(result[:], expanded[:])
+                nc.sync.dma_start(out[cb * P : (cb + 1) * P, q * TQ : (q + 1) * TQ], result[:])

@@ -35,12 +35,11 @@ def tile_qkvparallellinearwithlora_kernel(tc, x, a_w, b_pool, scale, mask, offs,
         mask_t = [held.tile([P, BLOCKS, TQ], F32, name=f"mask{q}") for q in range(CHUNKS)]
 
         nc.sync.dma_start(offsets[:], offs)
-        nc.sync.dma_start(pool_t[0][:], b_pool[0:P, :])
-        nc.scalar.dma_start(scale_t[0][:], scale[0:P, :])
         nc.sync.dma_start(a_t[:], blocked(a_w))
         nc.scalar.dma_start(x_t[:], blocked(x))
-        nc.sync.dma_start(pool_t[1][:], b_pool[P : 2 * P, :])
-        nc.scalar.dma_start(scale_t[1][:], scale[P : 2 * P, :])
+        for cb in range(BLOCKS):
+            nc.sync.dma_start(pool_t[cb][:], b_pool[cb * P : (cb + 1) * P, :])
+            nc.scalar.dma_start(scale_t[cb][:], scale[cb * P : (cb + 1) * P, :])
         nc.sync.dma_start(mask_t[0][:], blocked(mask)[:, :, 0:TQ])
         nc.scalar.dma_start(mask_t[1][:], blocked(mask)[:, :, TQ:T])
 
@@ -78,9 +77,9 @@ def tile_qkvparallellinearwithlora_kernel(tc, x, a_w, b_pool, scale, mask, offs,
                     )
             return shrunk
 
-        look_up(0)
         shrunk = [shrink(q) for q in range(CHUNKS)]
-        look_up(1)
+        for cb in range(BLOCKS):
+            look_up(cb)
 
         dm = []
         for q in range(CHUNKS):

@@ -29,17 +29,17 @@ def tile_qkvparallellinearwithlora_kernel(tc, x, a_w, b_pool, scale, mask, offs,
     ):
         offsets = held.tile([P, N // 16], U16, name="offsets")
         pool_t = [held.tile([P, S], F32, name=f"pool{cb}") for cb in range(BLOCKS)]
-        scale_t = [held.tile([P, N], F32, name=f"scale{cb}") for cb in range(BLOCKS)]
+        scale_t = held.tile([P, N], F32, name="scale_t")
         a_t = held.tile([P, BLOCKS, N], BF16, name="a_t")
         x_t = held.tile([P, BLOCKS, T], BF16, name="x_t")
         mask_t = [held.tile([P, BLOCKS, TQ], F32, name=f"mask{q}") for q in range(CHUNKS)]
 
         nc.sync.dma_start(offsets[:], offs)
+        nc.sync.dma_start(pool_t[0][:], b_pool[0:P, :])
+        nc.scalar.dma_start(scale_t[:], scale[0:P, :])
+        nc.scalar.dma_start(pool_t[1][:], b_pool[P : 2 * P, :])
         nc.sync.dma_start(a_t[:], blocked(a_w))
         nc.scalar.dma_start(x_t[:], blocked(x))
-        for cb in range(BLOCKS):
-            nc.sync.dma_start(pool_t[cb][:], b_pool[cb * P : (cb + 1) * P, :])
-            nc.scalar.dma_start(scale_t[cb][:], scale[cb * P : (cb + 1) * P, :])
         nc.sync.dma_start(mask_t[0][:], blocked(mask)[:, :, 0:TQ])
         nc.scalar.dma_start(mask_t[1][:], blocked(mask)[:, :, TQ:T])
 
@@ -48,38 +48,38 @@ def tile_qkvparallellinearwithlora_kernel(tc, x, a_w, b_pool, scale, mask, offs,
 
         zeros = held.tile([P, T], BF16, name="zeros")
         nc.vector.memset(zeros[:], 0.0)
-        idle_product = psum.tile([P, T], F32, name="idle_product")
+        shrunk = [psum.tile([P, BLOCKS, TQ], F32, name=f"shrunk{q}") for q in range(CHUNKS)]
         for i in range(WARM_UP_MATMULS):
-            nc.tensor.matmul(idle_product[:], zeros[:, :P], zeros[:], start=True, stop=True)
+            nc.tensor.matmul(
+                shrunk[0][:].rearrange("p b t -> p (b t)"), zeros[:, :P], zeros[:], start=True, stop=True
+            )
 
-        flipped = psum.tile([P, BLOCKS, BLOCKS, P], F32, name="flipped")
-        bwT = held.tile([P, BLOCKS, BLOCKS, P], BF16, name="bwT")
+        flipped = [psum.tile([P, BLOCKS, P], F32, name=f"flipped{cb}") for cb in range(BLOCKS)]
+        bwT = [held.tile([P, BLOCKS, P], BF16, name=f"bwT{cb}") for cb in range(BLOCKS)]
 
         def look_up(cb):
             bw = held.tile([P, BLOCKS, P], F32, name=f"bw{cb}")
             nc.vector.tensor_tensor(
-                bw[:].rearrange("p b j -> p (b j)"), pool_t[cb][:].indirect(offsets[:]), scale_t[cb][:], MULT
+                bw[:].rearrange("p b j -> p (b j)"), pool_t[cb][:].indirect(offsets[:]), scale_t[:], MULT
             )
             for jb in range(BLOCKS):
-                nc.tensor.transpose(flipped[:, cb, jb, :], bw[:, jb, :], identity[:])
-            nc.scalar.copy(bwT[:, cb], flipped[:, cb])
+                nc.tensor.transpose(flipped[cb][:, jb, :], bw[:, jb, :], identity[:])
+            nc.scalar.copy(bwT[cb][:], flipped[cb][:])
 
         def shrink(q):
-            shrunk = psum.tile([P, BLOCKS, TQ], F32, name=f"shrunk{q}")
             for jb in range(BLOCKS):
                 for kb in range(BLOCKS):
                     nc.tensor.matmul(
-                        shrunk[:, jb, :],
+                        shrunk[q][:, jb, :],
                         a_t[:, kb, jb * P : (jb + 1) * P],
                         x_t[:, kb, q * TQ : (q + 1) * TQ],
                         start=(kb == 0),
                         stop=(kb == BLOCKS - 1),
                     )
-            return shrunk
 
-        shrunk = [shrink(q) for q in range(CHUNKS)]
-        for cb in range(BLOCKS):
-            look_up(cb)
+        for i in range(BLOCKS):
+            look_up(i)
+            shrink(i)
 
         dm = []
         for q in range(CHUNKS):
@@ -93,7 +93,7 @@ def tile_qkvparallellinearwithlora_kernel(tc, x, a_w, b_pool, scale, mask, offs,
                 for jb in range(BLOCKS):
                     nc.tensor.matmul(
                         expanded[:],
-                        bwT[:, cb, jb, :],
+                        bwT[cb][:, jb, :],
                         dm[q][:, jb, :],
                         start=(jb == 0),
                         stop=(jb == BLOCKS - 1),

@@ -36,12 +36,12 @@ def tile_qkvparallellinearwithlora_kernel(tc, x, a_w, b_pool, scale, mask, offs,
 
         nc.sync.dma_start(offsets[:], offs)
         nc.sync.dma_start(pool_t[0][:], b_pool[0:P, :])
-        nc.scalar.dma_start(scale_t[:], scale[0:P, :])
-        nc.scalar.dma_start(pool_t[1][:], b_pool[P : 2 * P, :])
+        nc.sync.dma_start(scale_t[:], scale[0:P, :])
         nc.sync.dma_start(a_t[:], blocked(a_w))
-        nc.scalar.dma_start(x_t[:], blocked(x))
-        nc.sync.dma_start(mask_t[0][:], blocked(mask)[:, :, 0:TQ])
-        nc.scalar.dma_start(mask_t[1][:], blocked(mask)[:, :, TQ:T])
+        nc.sync.dma_start(x_t[:], blocked(x))
+        nc.sync.dma_start(pool_t[1][:], b_pool[P : 2 * P, :])
+        for q in range(CHUNKS):
+            nc.sync.dma_start(mask_t[q][:], blocked(mask)[:, :, q * TQ : (q + 1) * TQ])
 
         identity = held.tile([P, P], F32, name="identity")
         make_identity(nc, identity[:])
@@ -77,9 +77,10 @@ def tile_qkvparallellinearwithlora_kernel(tc, x, a_w, b_pool, scale, mask, offs,
                         stop=(kb == BLOCKS - 1),
                     )
 
-        for i in range(BLOCKS):
-            look_up(i)
-            shrink(i)
+        look_up(0)
+        for q in range(CHUNKS):
+            shrink(q)
+        look_up(1)
 
         dm = []
         for q in range(CHUNKS):

@@ -21,6 +21,10 @@ def blocked(rows):
     return rows.rearrange("(b p) w -> p b w", p=P)
 
 
+def paired(rows):
+    return rows.rearrange("(p b) w -> p b w", p=P)
+
+
 def tile_qkvparallellinearwithlora_kernel(tc, x, a_w, b_pool, scale, mask, offs, out):
     nc = tc.nc
     with (
@@ -37,8 +41,8 @@ def tile_qkvparallellinearwithlora_kernel(tc, x, a_w, b_pool, scale, mask, offs,
         nc.sync.dma_start(offsets[:], offs)
         nc.sync.dma_start(pool_t[0][:], b_pool[0:P, :])
         nc.sync.dma_start(scale_t[:], scale[0:P, :])
-        nc.sync.dma_start(a_t[:], blocked(a_w))
-        nc.sync.dma_start(x_t[:], blocked(x))
+        nc.sync.dma_start(a_t[:], paired(a_w))
+        nc.sync.dma_start(x_t[:], paired(x))
         nc.sync.dma_start(pool_t[1][:], b_pool[P : 2 * P, :])
         for q in range(CHUNKS):
             nc.sync.dma_start(mask_t[q][:], blocked(mask)[:, :, q * TQ : (q + 1) * TQ])

@@ -25,6 +25,10 @@ def paired(rows):
     return rows.rearrange("(p b) w -> p b w", p=P)
 
 
+def pieces(q):
+    return [(0, BLOCKS)] if q < CHUNKS - 1 else [(jb, jb + 1) for jb in range(BLOCKS)]
+
+
 def tile_qkvparallellinearwithlora_kernel(tc, x, a_w, b_pool, scale, mask, offs, out):
     nc = tc.nc
     with (
@@ -36,7 +40,9 @@ def tile_qkvparallellinearwithlora_kernel(tc, x, a_w, b_pool, scale, mask, offs,
         scale_t = held.tile([P, N], F32, name="scale_t")
         a_t = held.tile([P, BLOCKS, N], BF16, name="a_t")
         x_t = held.tile([P, BLOCKS, T], BF16, name="x_t")
-        mask_t = [held.tile([P, BLOCKS, TQ], F32, name=f"mask{q}") for q in range(CHUNKS)]
+        mask_t = {
+            (q, b0): held.tile([P, b1 - b0, TQ], F32, name=f"mask{q}{b0}") for q in range(CHUNKS) for b0, b1 in pieces(q)
+        }
 
         nc.sync.dma_start(offsets[:], offs)
         nc.sync.dma_start(pool_t[0][:], b_pool[0:P, :])
@@ -45,7 +51,8 @@ def tile_qkvparallellinearwithlora_kernel(tc, x, a_w, b_pool, scale, mask, offs,
         nc.sync.dma_start(x_t[:], paired(x))
         nc.sync.dma_start(pool_t[1][:], b_pool[P : 2 * P, :])
         for q in range(CHUNKS):
-            nc.sync.dma_start(mask_t[q][:], blocked(mask)[:, :, q * TQ : (q + 1) * TQ])
+            for b0, b1 in pieces(q):
+                nc.sync.dma_start(mask_t[q, b0][:], blocked(mask)[:, b0:b1, q * TQ : (q + 1) * TQ])
 
         identity = held.tile([P, P], F32, name="identity")
         make_identity(nc, identity[:])
@@ -86,26 +93,26 @@ def tile_qkvparallellinearwithlora_kernel(tc, x, a_w, b_pool, scale, mask, offs,
             shrink(q)
         look_up(1)
 
-        dm = []
+        expanded = [[psum.tile([P, TQ], F32, name=f"expanded{q}{cb}") for cb in range(BLOCKS)] for q in range(CHUNKS)]
         for q in range(CHUNKS):
-            kept = held.tile([P, BLOCKS, TQ], BF16, name=f"dm{q}")
-            nc.vector.tensor_tensor(kept[:], shrunk[q][:], mask_t[q][:], MULT)
-            dm.append(kept)
+            for b0, b1 in pieces(q):
+                dm = held.tile([P, b1 - b0, TQ], BF16, name=f"dm{q}{b0}")
+                nc.vector.tensor_tensor(dm[:], shrunk[q][:, b0:b1, :], mask_t[q, b0][:], MULT)
+                for jb in range(b0, b1):
+                    for cb in range(BLOCKS):
+                        nc.tensor.matmul(
+                            expanded[q][cb][:],
+                            bwT[cb][:, jb, :],
+                            dm[:, jb - b0, :],
+                            start=(jb == 0),
+                            stop=(jb == BLOCKS - 1),
+                        )
 
         for q in range(CHUNKS):
             for cb in range(BLOCKS):
-                expanded = psum.tile([P, TQ], F32, name=f"expanded{q}{cb}")
-                for jb in range(BLOCKS):
-                    nc.tensor.matmul(
-                        expanded[:],
-                        bwT[cb][:, jb, :],
-                        dm[q][:, jb, :],
-                        start=(jb == 0),
-                        stop=(jb == BLOCKS - 1),
-                    )
                 result = held.tile([P, TQ], F32, name=f"result{q}{cb}")
                 if cb == 0:
-                    nc.vector.tensor_copy(result[:], expanded[:])
+                    nc.vector.tensor_copy(result[:], expanded[q][cb][:])
                 else:
-                    nc.scalar.copy(result[:], expanded[:])
+                    nc.scalar.copy(result[:], expanded[q][cb][:])
                 nc.sync.dma_start(out[cb * P : (cb + 1) * P, q * TQ : (q + 1) * TQ], result[:])

@@ -7,7 +7,7 @@ S = 256
 N = 256
 T = 512
 BLOCKS = 2
-WARM_UP_MATMULS = 4
+WARM_UP_MATMULS = 2
 CHUNKS = 2
 TQ = T // CHUNKS
 
@@ -57,13 +57,19 @@ def tile_qkvparallellinearwithlora_kernel(tc, x, a_w, b_pool, scale, mask, offs,
         identity = held.tile([P, P], F32, name="identity")
         make_identity(nc, identity[:])
 
-        zeros = held.tile([P, T], BF16, name="zeros")
-        nc.vector.memset(zeros[:], 0.0)
+        zero_pairs = held.tile([P, T // 2], F32, name="zero_pairs")
+        nc.vector.memset(zero_pairs[:], 0.0)
+        zeros = zero_pairs[:].bitcast(BF16)
         shrunk = [psum.tile([P, BLOCKS, TQ], F32, name=f"shrunk{q}") for q in range(CHUNKS)]
         for i in range(WARM_UP_MATMULS):
-            nc.tensor.matmul(
-                shrunk[0][:].rearrange("p b t -> p (b t)"), zeros[:, :P], zeros[:], start=True, stop=True
-            )
+            for q in range(CHUNKS):
+                nc.tensor.matmul(
+                    shrunk[q][:].rearrange("p b t -> p (b t)"),
+                    identity[:].bitcast(BF16)[:, :P],
+                    zeros,
+                    start=True,
+                    stop=True,
+                )
 
         flipped = [psum.tile([P, BLOCKS, P], F32, name=f"flipped{cb}") for cb in range(BLOCKS)]
         bwT = [held.tile([P, BLOCKS, P], BF16, name=f"bwT{cb}") for cb in range(BLOCKS)]
@@ -98,8 +104,8 @@ def tile_qkvparallellinearwithlora_kernel(tc, x, a_w, b_pool, scale, mask, offs,
             for b0, b1 in pieces(q):
                 dm = held.tile([P, b1 - b0, TQ], BF16, name=f"dm{q}{b0}")
                 nc.vector.tensor_tensor(dm[:], shrunk[q][:, b0:b1, :], mask_t[q, b0][:], MULT)
-                for jb in range(b0, b1):
-                    for cb in range(BLOCKS):
+                for cb in range(BLOCKS):
+                    for jb in range(b0, b1):
                         nc.tensor.matmul(
                             expanded[q][cb][:],
                             bwT[cb][:, jb, :],

@@ -25,8 +25,7 @@ def paired(rows):
     return rows.rearrange("(p b) w -> p b w", p=P)
 
 
-def pieces(q):
-    return [(0, BLOCKS)] if q < CHUNKS - 1 else [(jb, jb + 1) for jb in range(BLOCKS)]
+PIECES = [(q, jb) for q in range(CHUNKS) for jb in range(BLOCKS)]
 
 
 def tile_qkvparallellinearwithlora_kernel(tc, x, a_w, b_pool, scale, mask, offs, out):
@@ -40,9 +39,7 @@ def tile_qkvparallellinearwithlora_kernel(tc, x, a_w, b_pool, scale, mask, offs,
         scale_t = held.tile([P, N], F32, name="scale_t")
         a_t = held.tile([P, BLOCKS, N], BF16, name="a_t")
         x_t = held.tile([P, BLOCKS, T], BF16, name="x_t")
-        mask_t = {
-            (q, b0): held.tile([P, b1 - b0, TQ], F32, name=f"mask{q}{b0}") for q in range(CHUNKS) for b0, b1 in pieces(q)
-        }
+        mask_t = {(q, jb): held.tile([P, TQ], F32, name=f"mask{q}{jb}") for q, jb in PIECES}
 
         nc.sync.dma_start(offsets[:], offs)
         nc.sync.dma_start(pool_t[0][:], b_pool[0:P, :])
@@ -50,9 +47,8 @@ def tile_qkvparallellinearwithlora_kernel(tc, x, a_w, b_pool, scale, mask, offs,
         nc.sync.dma_start(a_t[:], paired(a_w))
         nc.sync.dma_start(x_t[:], paired(x))
         nc.sync.dma_start(pool_t[1][:], b_pool[P : 2 * P, :])
-        for q in range(CHUNKS):
-            for b0, b1 in pieces(q):
-                nc.sync.dma_start(mask_t[q, b0][:], blocked(mask)[:, b0:b1, q * TQ : (q + 1) * TQ])
+        for q, jb in PIECES:
+            nc.sync.dma_start(mask_t[q, jb][:], blocked(mask)[:, jb, q * TQ : (q + 1) * TQ])
 
         identity = held.tile([P, P], F32, name="identity")
         make_identity(nc, identity[:])
@@ -100,19 +96,13 @@ def tile_qkvparallellinearwithlora_kernel(tc, x, a_w, b_pool, scale, mask, offs,
         look_up(1)
 
         expanded = [[psum.tile([P, TQ], F32, name=f"expanded{q}{cb}") for cb in range(BLOCKS)] for q in range(CHUNKS)]
-        for q in range(CHUNKS):
-            for b0, b1 in pieces(q):
-                dm = held.tile([P, b1 - b0, TQ], BF16, name=f"dm{q}{b0}")
-                nc.vector.tensor_tensor(dm[:], shrunk[q][:, b0:b1, :], mask_t[q, b0][:], MULT)
-                for cb in range(BLOCKS):
-                    for jb in range(b0, b1):
-                        nc.tensor.matmul(
-                            expanded[q][cb][:],
-                            bwT[cb][:, jb, :],
-                            dm[:, jb - b0, :],
-                            start=(jb == 0),
-                            stop=(jb == BLOCKS - 1),
-                        )
+        for q, jb in PIECES:
+            dm = held.tile([P, TQ], BF16, name=f"dm{q}{jb}")
+            nc.vector.tensor_tensor(dm[:], shrunk[q][:, jb, :], mask_t[q, jb][:], MULT)
+            for cb in range(BLOCKS):
+                nc.tensor.matmul(
+                    expanded[q][cb][:], bwT[cb][:, jb, :], dm[:], start=(jb == 0), stop=(jb == BLOCKS - 1)
+                )
 
         for q in range(CHUNKS):
             for cb in range(BLOCKS):

@@ -45,8 +45,8 @@ def tile_qkvparallellinearwithlora_kernel(tc, x, a_w, b_pool, scale, mask, offs,
         nc.sync.dma_start(pool_t[0][:], b_pool[0:P, :])
         nc.sync.dma_start(scale_t[:], scale[0:P, :])
         nc.sync.dma_start(a_t[:], paired(a_w))
-        nc.sync.dma_start(x_t[:], paired(x))
         nc.sync.dma_start(pool_t[1][:], b_pool[P : 2 * P, :])
+        nc.sync.dma_start(x_t[:], paired(x))
         for q, jb in PIECES:
             nc.sync.dma_start(mask_t[q, jb][:], blocked(mask)[:, jb, q * TQ : (q + 1) * TQ])
 

@@ -53,19 +53,13 @@ def tile_qkvparallellinearwithlora_kernel(tc, x, a_w, b_pool, scale, mask, offs,
         identity = held.tile([P, P], F32, name="identity")
         make_identity(nc, identity[:])
 
-        zero_pairs = held.tile([P, T // 2], F32, name="zero_pairs")
+        zero_pairs = held.tile([P, TQ // 2], F32, name="zero_pairs")
         nc.vector.memset(zero_pairs[:], 0.0)
         zeros = zero_pairs[:].bitcast(BF16)
-        shrunk = [psum.tile([P, BLOCKS, TQ], F32, name=f"shrunk{q}") for q in range(CHUNKS)]
+        shrunk = {(q, jb): psum.tile([P, TQ], F32, name=f"shrunk{q}{jb}") for q, jb in PIECES}
         for i in range(WARM_UP_MATMULS):
-            for q in range(CHUNKS):
-                nc.tensor.matmul(
-                    shrunk[q][:].rearrange("p b t -> p (b t)"),
-                    identity[:].bitcast(BF16)[:, :P],
-                    zeros,
-                    start=True,
-                    stop=True,
-                )
+            for piece in PIECES:
+                nc.tensor.matmul(shrunk[piece][:], identity[:].bitcast(BF16)[:, :P], zeros, start=True, stop=True)
 
         flipped = [psum.tile([P, BLOCKS, P], F32, name=f"flipped{cb}") for cb in range(BLOCKS)]
         bwT = [held.tile([P, BLOCKS, P], BF16, name=f"bwT{cb}") for cb in range(BLOCKS)]
@@ -79,26 +73,29 @@ def tile_qkvparallellinearwithlora_kernel(tc, x, a_w, b_pool, scale, mask, offs,
                 nc.tensor.transpose(flipped[cb][:, jb, :], bw[:, jb, :], identity[:])
             nc.scalar.copy(bwT[cb][:], flipped[cb][:])
 
-        def shrink(q):
-            for jb in range(BLOCKS):
-                for kb in range(BLOCKS):
-                    nc.tensor.matmul(
-                        shrunk[q][:, jb, :],
-                        a_t[:, kb, jb * P : (jb + 1) * P],
-                        x_t[:, kb, q * TQ : (q + 1) * TQ],
-                        start=(kb == 0),
-                        stop=(kb == BLOCKS - 1),
-                    )
+        def shrink(q, jb):
+            for kb in range(BLOCKS):
+                nc.tensor.matmul(
+                    shrunk[q, jb][:],
+                    a_t[:, kb, jb * P : (jb + 1) * P],
+                    x_t[:, kb, q * TQ : (q + 1) * TQ],
+                    start=(kb == 0),
+                    stop=(kb == BLOCKS - 1),
+                )
 
-        look_up(0)
-        for q in range(CHUNKS):
-            shrink(q)
-        look_up(1)
+        for half in range(BLOCKS):
+            look_up(half)
+            for q, jb in PIECES:
+                if q == half:
+                    shrink(q, jb)
 
-        expanded = [[psum.tile([P, TQ], F32, name=f"expanded{q}{cb}") for cb in range(BLOCKS)] for q in range(CHUNKS)]
+        bank = [["expanded0", "expanded1"], ["flipped0", "flipped1"]]
+        expanded = [
+            [psum.tile([P, TQ], F32, name=f"expanded{q}{cb}", tag=bank[q][cb]) for cb in range(BLOCKS)] for q in range(CHUNKS)
+        ]
         for q, jb in PIECES:
             dm = held.tile([P, TQ], BF16, name=f"dm{q}{jb}")
-            nc.vector.tensor_tensor(dm[:], shrunk[q][:, jb, :], mask_t[q, jb][:], MULT)
+            nc.vector.tensor_tensor(dm[:], shrunk[q, jb][:], mask_t[q, jb][:], MULT)
             for cb in range(BLOCKS):
                 nc.tensor.matmul(
                     expanded[q][cb][:], bwT[cb][:, jb, :], dm[:], start=(jb == 0), stop=(jb == BLOCKS - 1)

@@ -89,23 +89,32 @@ def tile_qkvparallellinearwithlora_kernel(tc, x, a_w, b_pool, scale, mask, offs,
                 if q == half:
                     shrink(q, jb)
 
-        bank = [["expanded0", "expanded1"], ["flipped0", "flipped1"]]
-        expanded = [
-            [psum.tile([P, TQ], F32, name=f"expanded{q}{cb}", tag=bank[q][cb]) for cb in range(BLOCKS)] for q in range(CHUNKS)
-        ]
+        halves = [(0, TQ // 2), (TQ // 2, TQ)]
+        whole = [(0, TQ)]
+        parts = [(0, cb, t0, t1, f"expanded{cb}") for cb in range(BLOCKS) for t0, t1 in whole]
+        parts += [(1, cb, t0, t1, f"flipped{cb}" if t0 == 0 else f"shrunk0{cb}") for cb in range(BLOCKS) for t0, t1 in halves]
+        expanded = {
+            (q, cb, t0, t1): psum.tile([P, t1 - t0], F32, name=f"expanded{q}{cb}{t0}", tag=bank) for q, cb, t0, t1, bank in parts
+        }
         for q, jb in PIECES:
             dm = held.tile([P, TQ], BF16, name=f"dm{q}{jb}")
             nc.vector.tensor_tensor(dm[:], shrunk[q, jb][:], mask_t[q, jb][:], MULT)
             for cb in range(BLOCKS):
-                nc.tensor.matmul(
-                    expanded[q][cb][:], bwT[cb][:, jb, :], dm[:], start=(jb == 0), stop=(jb == BLOCKS - 1)
-                )
+                for t0, t1 in whole if q == 0 else halves:
+                    nc.tensor.matmul(
+                        expanded[q, cb, t0, t1][:],
+                        bwT[cb][:, jb, :],
+                        dm[:, t0:t1],
+                        start=(jb == 0),
+                        stop=(jb == BLOCKS - 1),
+                    )
 
         for q in range(CHUNKS):
             for cb in range(BLOCKS):
                 result = held.tile([P, TQ], F32, name=f"result{q}{cb}")
-                if cb == 0:
-                    nc.vector.tensor_copy(result[:], expanded[q][cb][:])
-                else:
-                    nc.scalar.copy(result[:], expanded[q][cb][:])
+                for t0, t1 in whole if q == 0 else halves:
+                    if (cb if q == 0 else t0) == 0:
+                        nc.vector.tensor_copy(result[:, t0:t1], expanded[q, cb, t0, t1][:])
+                    else:
+                        nc.scalar.copy(result[:, t0:t1], expanded[q, cb, t0, t1][:])
                 nc.sync.dma_start(out[cb * P : (cb + 1) * P, q * TQ : (q + 1) * TQ], result[:])

import concourse.mybir as mybir
from concourse.masks import make_identity

P = 128
C = 256
S = 256
N = 256
T = 512
BLOCKS = 2
WARM_UP_MATMULS = 2
CHUNKS = 2
TQ = T // CHUNKS

FLOPS = 2 * C * N * T + 2 * N * C * T

BF16, F32, U16 = mybir.dt.bfloat16, mybir.dt.float32, mybir.dt.uint16
MULT = mybir.AluOpType.mult


def blocked(rows):
    return rows.rearrange("(b p) w -> p b w", p=P)


def paired(rows):
    return rows.rearrange("(p b) w -> p b w", p=P)


PIECES = [(q, jb) for q in range(CHUNKS) for jb in range(BLOCKS)]


def tile_qkvparallellinearwithlora_kernel(tc, x, a_w, b_pool, scale, mask, offs, out):
    nc = tc.nc
    with (
        tc.tile_pool(name="held", bufs=1) as held,
        tc.psum_pool(name="psum", bufs=1) as psum,
    ):
        offsets = held.tile([P, N // 16], U16, name="offsets")
        pool_t = [held.tile([P, S], F32, name=f"pool{cb}") for cb in range(BLOCKS)]
        scale_t = held.tile([P, N], F32, name="scale_t")
        a_t = held.tile([P, BLOCKS, N], BF16, name="a_t")
        x_t = held.tile([P, BLOCKS, T], BF16, name="x_t")
        mask_t = {(q, jb): held.tile([P, TQ], F32, name=f"mask{q}{jb}") for q, jb in PIECES}

        nc.sync.dma_start(offsets[:], offs)
        nc.sync.dma_start(pool_t[0][:], b_pool[0:P, :])
        nc.sync.dma_start(scale_t[:], scale[0:P, :])
        nc.sync.dma_start(a_t[:], paired(a_w))
        nc.sync.dma_start(pool_t[1][:], b_pool[P : 2 * P, :])
        nc.sync.dma_start(x_t[:], paired(x))
        for q, jb in PIECES:
            nc.sync.dma_start(mask_t[q, jb][:], blocked(mask)[:, jb, q * TQ : (q + 1) * TQ])

        identity = held.tile([P, P], F32, name="identity")
        make_identity(nc, identity[:])

        zero_pairs = held.tile([P, TQ // 2], F32, name="zero_pairs")
        nc.vector.memset(zero_pairs[:], 0.0)
        zeros = zero_pairs[:].bitcast(BF16)
        shrunk = {(q, jb): psum.tile([P, TQ], F32, name=f"shrunk{q}{jb}") for q, jb in PIECES}
        for i in range(WARM_UP_MATMULS):
            for piece in PIECES:
                nc.tensor.matmul(shrunk[piece][:], identity[:].bitcast(BF16)[:, :P], zeros, start=True, stop=True)

        flipped = [psum.tile([P, BLOCKS, P], F32, name=f"flipped{cb}") for cb in range(BLOCKS)]
        bwT = [held.tile([P, BLOCKS, P], BF16, name=f"bwT{cb}") for cb in range(BLOCKS)]

        def look_up(cb):
            bw = held.tile([P, BLOCKS, P], F32, name=f"bw{cb}")
            nc.vector.tensor_tensor(
                bw[:].rearrange("p b j -> p (b j)"), pool_t[cb][:].indirect(offsets[:]), scale_t[:], MULT
            )
            for jb in range(BLOCKS):
                nc.tensor.transpose(flipped[cb][:, jb, :], bw[:, jb, :], identity[:])
            nc.scalar.copy(bwT[cb][:], flipped[cb][:])

        def shrink(q, jb):
            for kb in range(BLOCKS):
                nc.tensor.matmul(
                    shrunk[q, jb][:],
                    a_t[:, kb, jb * P : (jb + 1) * P],
                    x_t[:, kb, q * TQ : (q + 1) * TQ],
                    start=(kb == 0),
                    stop=(kb == BLOCKS - 1),
                )

        for half in range(BLOCKS):
            look_up(half)
            for q, jb in PIECES:
                if q == half:
                    shrink(q, jb)

        halves = [(0, TQ // 2), (TQ // 2, TQ)]
        whole = [(0, TQ)]
        parts = [(0, cb, t0, t1, f"expanded{cb}") for cb in range(BLOCKS) for t0, t1 in whole]
        parts += [(1, cb, t0, t1, f"flipped{cb}" if t0 == 0 else f"shrunk0{cb}") for cb in range(BLOCKS) for t0, t1 in halves]
        expanded = {
            (q, cb, t0, t1): psum.tile([P, t1 - t0], F32, name=f"expanded{q}{cb}{t0}", tag=bank) for q, cb, t0, t1, bank in parts
        }
        for q, jb in PIECES:
            dm = held.tile([P, TQ], BF16, name=f"dm{q}{jb}")
            nc.vector.tensor_tensor(dm[:], shrunk[q, jb][:], mask_t[q, jb][:], MULT)
            for cb in range(BLOCKS):
                for t0, t1 in whole if q == 0 else halves:
                    nc.tensor.matmul(
                        expanded[q, cb, t0, t1][:],
                        bwT[cb][:, jb, :],
                        dm[:, t0:t1],
                        start=(jb == 0),
                        stop=(jb == BLOCKS - 1),
                    )

        for q in range(CHUNKS):
            for cb in range(BLOCKS):
                result = held.tile([P, TQ], F32, name=f"result{q}{cb}")
                for t0, t1 in whole if q == 0 else halves:
                    if (cb if q == 0 else t0) == 0:
                        nc.vector.tensor_copy(result[:, t0:t1], expanded[q, cb, t0, t1][:])
                    else:
                        nc.scalar.copy(result[:, t0:t1], expanded[q, cb, t0, t1][:])
                nc.sync.dma_start(out[cb * P : (cb + 1) * P, q * TQ : (q + 1) * TQ], result[:])
